import numpy as np
import ml_dtypes


def mxq(x, axis, fmt="e4m3"):
    dtype, down = {"e4m3": (ml_dtypes.float8_e4m3fn, 7), "e5m2": (ml_dtypes.float8_e5m2, 14)}[fmt]
    v = np.moveaxis(np.asarray(x, np.float32).astype(ml_dtypes.bfloat16).astype(np.float64), axis, -1)
    blocks = v.reshape(v.shape[:-1] + (-1, 32))
    amax = np.abs(blocks).max(-1, keepdims=True)
    byte = np.maximum(np.where(amax > 0, np.frexp(amax)[1] - 1 + 127, 0) - down, 1)
    scale = np.exp2(byte - 127.0)
    codes = (blocks / scale).astype(np.float32).astype(dtype).astype(np.float64)
    return np.moveaxis((codes * scale).reshape(v.shape), -1, axis)


WIDE = False


def mx_kscale(k):
    if not WIDE:
        return np.ones(k)
    levels = np.array([10, -10, 5, -5, 0])
    a = np.random.permutation(np.resize(levels, k // 512 * 4)).reshape(k // 512, 4)
    idx = np.arange(k)
    return np.exp2(a[idx // 512, idx % 128 // 32])


BF16 = ml_dtypes.bfloat16


def bf(x):
    return np.asarray(x, np.float32).astype(BF16)


def f64(x):
    return np.asarray(x).astype(np.float64)


B, CL, CH, CK, CV, CO, H, W = 2, 1024, 512, 256, 512, 512, 48, 72
N = H * W
CF = CO + CH
EPS = 1e-5


def setup_inputs():
    s = mx_kscale(CV)
    t = mx_kscale(CF)
    tc, th = t[:CO], t[CO:]
    return {"context": bf(np.random.standard_normal((B, CV, H, W)) * 0.4 * s[None, :, None, None]),
            "high_feats": bf(np.random.standard_normal((B, CH, H, W)) * th[None, :, None, None]),
            "ww": bf(np.random.standard_normal((CO, CV)) * 2.0 / np.sqrt(CV) / s[None, :] * tc[:, None]),
            "bw": bf(np.random.standard_normal(CO) * 0.3 * tc),
            "wf": bf(np.random.standard_normal((CO, CF)) / np.sqrt(CF) / t[None, :]),
            "bfuse": bf(np.random.standard_normal(CO) * 0.3),
            "gf": bf(np.random.uniform(0.5, 1.5, CO)),
            "bef": bf(np.random.standard_normal(CO) * 0.3),
            "mf": bf(np.random.standard_normal(CO) * 0.3),
            "vf": bf(np.random.uniform(0.5, 1.5, CO))}


def reference(context, high_feats, ww, bw, wf, bfuse, gf, bef, mf, vf):
    ctx = f64(context).reshape(B, CV, N)
    hi = f64(high_feats).reshape(B, CH, N)
    c = (mxq(f64(ww), 1, "e4m3") @ mxq(ctx, 1, "e4m3")) + f64(bw)[None, :, None]
    fused = np.concatenate([c, hi], axis=1)
    y = (mxq(f64(wf), 1, "e4m3") @ mxq(fused, 1, "e4m3")) + f64(bfuse)[None, :, None]
    sc = f64(gf) / np.sqrt(f64(vf) + EPS)
    out = (y - f64(mf)[None, :, None]) * sc[None, :, None] + f64(bef)[None, :, None]
    return out.reshape(B, CO, H, W)

@@ -1,0 +1,221 @@
+from contextlib import ExitStack
+
+import concourse.mybir as mybir
+from concourse.masks import make_identity
+
+F32 = mybir.dt.float32
+BF16 = mybir.dt.bfloat16
+U32 = mybir.dt.uint32
+U8 = mybir.dt.uint8
+FP8X4 = mybir.dt.float8_e4m3fn_x4
+IDENTITY = mybir.ActivationFunctionType.Identity
+
+P = 128
+PACK = 4
+K_PASS = P * PACK
+
+BATCH, PIXELS = 2, 48 * 72
+CV, CH, CO = 512, 512, 512
+COLS = BATCH * PIXELS
+CHUNK = 512
+M_TILES = CO // P
+LOAD_COLS = 2 * CHUNK
+RUN = 4
+LAG = 2
+EPS = 1e-5
+
+FLOPS = 2 * COLS * (CO * CV + CO * (CO + CH))
+
+
+def batch_parts(first, last):
+    parts = []
+    for b in range(BATCH):
+        lo = max(first, b * PIXELS)
+        hi = min(last, (b + 1) * PIXELS)
+        if lo < hi:
+            parts.append((b, lo - b * PIXELS, hi - b * PIXELS))
+    return parts
+
+
+def tile_afnb_pb_t_kernel(tc, context, high_feats, ww, bw, wf, bfuse, gf, bef, mf, vf, out):
+    nc = tc.nc
+    chunks = [(first, min(CHUNK, COLS - first)) for first in range(0, COLS, CHUNK)]
+    rounds = len(chunks)
+
+    ctx_rows = context.rearrange("b (p j) h w -> b p j (h w)", j=PACK)
+    hi_rows = high_feats.rearrange("b (p j) h w -> b p j (h w)", j=PACK)
+    out_rows = out.rearrange("b (p m) h w -> b p m (h w)", m=M_TILES)
+
+    with ExitStack() as stack:
+        keep = stack.enter_context(tc.tile_pool(name="keep", bufs=1))
+        work = stack.enter_context(tc.tile_pool(name="work", bufs=2))
+        psum = stack.enter_context(tc.psum_pool(name="psum", bufs=4))
+
+        ww_sb = keep.tile([P, M_TILES * CV], BF16)
+        wf_sb = keep.tile([P, M_TILES * (CO + CH)], BF16)
+        ctx_raw = keep.tile([P, PACK, COLS], BF16)
+        hi_raw = keep.tile([P, PACK, COLS], BF16)
+
+        def load_columns(raw, rows, first, last):
+            for b, n0, n1 in batch_parts(first, last):
+                col = b * PIXELS + n0
+                nc.sync.dma_start(out=raw[:, :, col : col + n1 - n0], in_=rows[b, :, :, n0:n1])
+
+        nc.sync.dma_start(out=ww_sb[:], in_=ww.rearrange("(p m) k -> p (m k)", m=M_TILES))
+        load_columns(ctx_raw, ctx_rows, 0, CHUNK)
+        load_columns(hi_raw, hi_rows, 0, CHUNK)
+        nc.sync.dma_start(out=wf_sb[:], in_=wf.rearrange("(p m) k -> p (m k)", m=M_TILES))
+        for first in range(CHUNK, COLS, LOAD_COLS):
+            load_columns(ctx_raw, ctx_rows, first, min(first + LOAD_COLS, COLS))
+            load_columns(hi_raw, hi_rows, first, min(first + LOAD_COLS, COLS))
+
+        def load_vector(vec, name):
+            vec_sb = keep.tile([P, M_TILES], BF16, name=name)
+            nc.scalar.dma_start(out=vec_sb[:], in_=vec.rearrange("(p m) -> p m", m=M_TILES))
+            return vec_sb
+
+        bw_sb = load_vector(bw, "bw_sb")
+        vf_sb = load_vector(vf, "vf_sb")
+        gf_sb = load_vector(gf, "gf_sb")
+        bfuse_sb = load_vector(bfuse, "bfuse_sb")
+        mf_sb = load_vector(mf, "mf_sb")
+        bef_sb = load_vector(bef, "bef_sb")
+
+        ident = keep.tile([P, P], F32)
+        make_identity(nc, ident[:])
+
+        def regroup(grouped, planes):
+            nc.vector.tensor_copy(
+                out=grouped.rearrange("p (c i) t -> p c t i", i=RUN),
+                in_=planes.rearrange("p t (c i) -> p c t i", i=RUN),
+            )
+
+        def quantise(grouped, codes, scales):
+            nc.vector.quantize_mx(out=codes.bitcast(FP8X4), scales=scales, in_=grouped)
+
+        def quantise_weight(w_sb, passes, name):
+            words = w_sb[:].bitcast(F32).rearrange("p (m g q u) -> p m g u q", m=M_TILES, g=passes, u=2)
+            grouped = keep.tile([P, passes * M_TILES * P * PACK], BF16, align_bytes=64, name=name + "_grouped")
+            pairs = grouped[:].bitcast(F32).rearrange("q (g m c u) -> q g m c u", g=passes, m=M_TILES, u=2)
+            for g in range(passes):
+                for m0 in range(0, M_TILES, 2):
+                    bank = psum.tile([P, 2, 2, P], F32, name="w_bank", tag="y_acc")
+                    for i in range(2):
+                        for u in range(2):
+                            nc.tensor.transpose(bank[:, i, u, :], words[:, m0 + i, g, u, :], ident[:])
+                    nc.scalar.copy(out=pairs[:, g, m0 : m0 + 2], in_=bank[:].rearrange("q i u c -> q i c u"))
+            codes = keep.tile([P, passes, M_TILES, P], U32, align_bytes=64, name=name + "_codes")
+            scales = keep.tile([P, passes, M_TILES, P], U8, align_bytes=64, name=name + "_scales")
+            quantise(
+                grouped[:],
+                codes[:].rearrange("q g m c -> q (g m c)"),
+                scales[:].rearrange("q g m c -> q (g m c)"),
+            )
+            return codes, scales
+
+        ctx_grouped, hi_grouped, c_grouped = {}, {}, {}
+        hi_codes, hi_scales, c_planes = {}, {}, {}
+
+        def regroup_inputs(i):
+            first, width = chunks[i]
+            ctx_grouped[i] = work.tile([P, CHUNK, PACK], BF16, align_bytes=64, name="ctx_grouped")
+            regroup(ctx_grouped[i][:, :width, :], ctx_raw[:, :, first : first + width])
+            hi_grouped[i] = work.tile([P, CHUNK, PACK], BF16, align_bytes=64, name="hi_grouped")
+            regroup(hi_grouped[i][:, :width, :], hi_raw[:, :, first : first + width])
+
+        def first_product(i):
+            width = chunks[i][1]
+            ctx_codes = work.tile([P, CHUNK], U32, align_bytes=64)
+            ctx_scales = work.tile([P, CHUNK], U8, align_bytes=64)
+            quantise(
+                ctx_grouped[i][:, :width, :].rearrange("p n t -> p (n t)"),
+                ctx_codes[:, :width],
+                ctx_scales[:, :width],
+            )
+            c_planes[i] = work.tile([P, M_TILES, CHUNK], BF16, name="c_planes", bufs=LAG + 1)
+            for m in range(M_TILES):
+                c_acc = psum.tile([P, CHUNK], F32)
+                nc.tensor.matmul_mx(
+                    out=c_acc[:, :width],
+                    lhsT=ww_codes[:, 0, m, :].bitcast(FP8X4),
+                    lhsT_scale=ww_scales[:, 0, m, :],
+                    rhs=ctx_codes[:, :width].bitcast(FP8X4),
+                    rhs_scale=ctx_scales[:, :width],
+                    start=True,
+                    stop=True,
+                )
+                nc.scalar.activation(
+                    out=c_planes[i][:, m, :width], in_=c_acc[:, :width], func=IDENTITY, bias=bw_f32[:, m : m + 1], scale=1.0
+                )
+            if i + 1 < rounds:
+                regroup_inputs(i + 1)
+            hi_codes[i] = work.tile([P, CHUNK], U32, align_bytes=64, name="hi_codes", bufs=LAG + 1)
+            hi_scales[i] = work.tile([P, CHUNK], U8, align_bytes=64, name="hi_scales", bufs=LAG + 1)
+            quantise(
+                hi_grouped[i][:, :width, :].rearrange("p n t -> p (n t)"),
+                hi_codes[i][:, :width],
+                hi_scales[i][:, :width],
+            )
+
+        def regroup_c(i):
+            width = chunks[i][1]
+            c_grouped[i] = work.tile([P, CHUNK, PACK], BF16, align_bytes=64, name="c_grouped")
+            regroup(c_grouped[i][:, :width, :], c_planes[i][:, :, :width])
+
+        def second_product(i):
+            first, width = chunks[i]
+            c_codes = work.tile([P, CHUNK], U32, align_bytes=64)
+            c_scales = work.tile([P, CHUNK], U8, align_bytes=64)
+            quantise(
+                c_grouped[i][:, :width, :].rearrange("p n t -> p (n t)"), c_codes[:, :width], c_scales[:, :width]
+            )
+            moving = [(c_codes, c_scales), (hi_codes[i], hi_scales[i])]
+            y_sb = work.tile([P, M_TILES, CHUNK], F32, bufs=3)
+            for m in range(M_TILES):
+                y_acc = psum.tile([P, CHUNK], F32)
+                for g in (1, 0):
+                    nc.tensor.matmul_mx(
+                        out=y_acc[:, :width],
+                        lhsT=wf_codes[:, g, m, :].bitcast(FP8X4),
+                        lhsT_scale=wf_scales[:, g, m, :],
+                        rhs=moving[g][0][:, :width].bitcast(FP8X4),
+                        rhs_scale=moving[g][1][:, :width],
+                        start=(g == 1),
+                        stop=(g == 0),
+                    )
+                nc.scalar.activation(
+                    out=y_sb[:, m, :width],
+                    in_=y_acc[:, :width],
+                    func=IDENTITY,
+                    scale=bn_scale[:, m : m + 1],
+                    bias=bn_shift[:, m : m + 1],
+                )
+            for b, n0, n1 in batch_parts(first, first + width):
+                col = b * PIXELS + n0 - first
+                nc.sync.dma_start(out=out_rows[b, :, :, n0:n1], in_=y_sb[:, :, col : col + n1 - n0])
+
+        bw_f32 = keep.tile([P, M_TILES], F32)
+        nc.vector.tensor_copy(out=bw_f32[:], in_=bw_sb[:])
+        regroup_inputs(0)
+        ww_codes, ww_scales = quantise_weight(ww_sb, CV // K_PASS, "ww")
+
+        bn_scale = keep.tile([P, M_TILES], F32)
+        bn_shift = keep.tile([P, M_TILES], F32)
+        nc.vector.tensor_scalar_add(out=bn_scale[:], in0=vf_sb[:], scalar1=EPS)
+        nc.scalar.sqrt(out=bn_scale[:], in_=bn_scale[:])
+        nc.vector.reciprocal(out=bn_scale[:], in_=bn_scale[:])
+        nc.vector.tensor_mul(out=bn_scale[:], in0=bn_scale[:], in1=gf_sb[:])
+        nc.vector.tensor_sub(out=bn_shift[:], in0=bfuse_sb[:], in1=mf_sb[:])
+        nc.vector.tensor_mul(out=bn_shift[:], in0=bn_shift[:], in1=bn_scale[:])
+        nc.vector.tensor_add(out=bn_shift[:], in0=bn_shift[:], in1=bef_sb[:])
+
+        for i in range(LAG):
+            first_product(i)
+        wf_codes, wf_scales = quantise_weight(wf_sb, (CO + CH) // K_PASS, "wf")
+        for i in range(LAG, rounds):
+            regroup_c(i - LAG)
+            first_product(i)
+            second_product(i - LAG)
+        for i in range(rounds - LAG, rounds):
+            regroup_c(i)
+            second_product(i)

@@ -53,21 +53,23 @@ def tile_afnb_pb_t_kernel(tc, context, high_feats, ww, bw, wf, bfuse, gf, bef, m
 
         ww_sb = keep.tile([P, M_TILES * CV], BF16)
         wf_sb = keep.tile([P, M_TILES * (CO + CH)], BF16)
-        ctx_raw = keep.tile([P, PACK, COLS], BF16)
-        hi_raw = keep.tile([P, PACK, COLS], BF16)
+        ctx_raw, hi_raw = {}, {}
 
-        def load_columns(raw, rows, first, last):
+        def load_columns(raw, rows, name, first, last):
+            raw[first] = keep.tile([P, PACK, last - first], BF16, name="%s_%d" % (name, first))
             for b, n0, n1 in batch_parts(first, last):
-                col = b * PIXELS + n0
-                nc.sync.dma_start(out=raw[:, :, col : col + n1 - n0], in_=rows[b, :, :, n0:n1])
+                col = b * PIXELS + n0 - first
+                nc.sync.dma_start(out=raw[first][:, :, col : col + n1 - n0], in_=rows[b, :, :, n0:n1])
 
+        load_starts = [0] + list(range(CHUNK, COLS, LOAD_COLS))
+        load_ends = load_starts[1:] + [COLS]
         nc.sync.dma_start(out=ww_sb[:], in_=ww.rearrange("(p m) k -> p (m k)", m=M_TILES))
-        load_columns(ctx_raw, ctx_rows, 0, CHUNK)
-        load_columns(hi_raw, hi_rows, 0, CHUNK)
+        load_columns(ctx_raw, ctx_rows, "ctx_raw", load_starts[0], load_ends[0])
+        load_columns(hi_raw, hi_rows, "hi_raw", load_starts[0], load_ends[0])
         nc.sync.dma_start(out=wf_sb[:], in_=wf.rearrange("(p m) k -> p (m k)", m=M_TILES))
-        for first in range(CHUNK, COLS, LOAD_COLS):
-            load_columns(ctx_raw, ctx_rows, first, min(first + LOAD_COLS, COLS))
-            load_columns(hi_raw, hi_rows, first, min(first + LOAD_COLS, COLS))
+        for first, last in zip(load_starts[1:], load_ends[1:]):
+            load_columns(ctx_raw, ctx_rows, "ctx_raw", first, last)
+            load_columns(hi_raw, hi_rows, "hi_raw", first, last)
 
         def load_vector(vec, name):
             vec_sb = keep.tile([P, M_TILES], BF16, name=name)
@@ -118,10 +120,12 @@ def tile_afnb_pb_t_kernel(tc, context, high_feats, ww, bw, wf, bfuse, gf, bef, m
 
         def regroup_inputs(i):
             first, width = chunks[i]
+            load = max(start for start in load_starts if start <= first)
+            col = first - load
             ctx_grouped[i] = work.tile([P, CHUNK, PACK], BF16, align_bytes=64, name="ctx_grouped")
-            regroup(ctx_grouped[i][:, :width, :], ctx_raw[:, :, first : first + width])
+            regroup(ctx_grouped[i][:, :width, :], ctx_raw[load][:, :, col : col + width])
             hi_grouped[i] = work.tile([P, CHUNK, PACK], BF16, align_bytes=64, name="hi_grouped")
-            regroup(hi_grouped[i][:, :width, :], hi_raw[:, :, first : first + width])
+            regroup(hi_grouped[i][:, :width, :], hi_raw[load][:, :, col : col + width])
 
         def first_product(i):
             width = chunks[i][1]
@@ -196,21 +200,21 @@ def tile_afnb_pb_t_kernel(tc, context, high_feats, ww, bw, wf, bfuse, gf, bef, m
 
         bw_f32 = keep.tile([P, M_TILES], F32)
         nc.vector.tensor_copy(out=bw_f32[:], in_=bw_sb[:])
-        regroup_inputs(0)
-        ww_codes, ww_scales = quantise_weight(ww_sb, CV // K_PASS, "ww")
-
         bn_scale = keep.tile([P, M_TILES], F32)
         bn_shift = keep.tile([P, M_TILES], F32)
         nc.vector.tensor_scalar_add(out=bn_scale[:], in0=vf_sb[:], scalar1=EPS)
         nc.scalar.sqrt(out=bn_scale[:], in_=bn_scale[:])
+
+        regroup_inputs(0)
+        ww_codes, ww_scales = quantise_weight(ww_sb, CV // K_PASS, "ww")
+        for i in range(LAG):
+            first_product(i)
+
         nc.vector.reciprocal(out=bn_scale[:], in_=bn_scale[:])
         nc.vector.tensor_mul(out=bn_scale[:], in0=bn_scale[:], in1=gf_sb[:])
         nc.vector.tensor_sub(out=bn_shift[:], in0=bfuse_sb[:], in1=mf_sb[:])
         nc.vector.tensor_mul(out=bn_shift[:], in0=bn_shift[:], in1=bn_scale[:])
         nc.vector.tensor_add(out=bn_shift[:], in0=bn_shift[:], in1=bef_sb[:])
-
-        for i in range(LAG):
-            first_product(i)
         wf_codes, wf_scales = quantise_weight(wf_sb, (CO + CH) // K_PASS, "wf")
         for i in range(LAG, rounds):
             regroup_c(i - LAG)

@@ -63,8 +63,8 @@ def tile_afnb_pb_t_kernel(tc, context, high_feats, ww, bw, wf, bfuse, gf, bef, m
 
         load_starts = [0] + list(range(CHUNK, COLS, LOAD_COLS))
         load_ends = load_starts[1:] + [COLS]
-        nc.sync.dma_start(out=ww_sb[:], in_=ww.rearrange("(p m) k -> p (m k)", m=M_TILES))
         load_columns(ctx_raw, ctx_rows, "ctx_raw", load_starts[0], load_ends[0])
+        nc.sync.dma_start(out=ww_sb[:], in_=ww.rearrange("(p m) k -> p (m k)", m=M_TILES))
         load_columns(hi_raw, hi_rows, "hi_raw", load_starts[0], load_ends[0])
         nc.sync.dma_start(out=wf_sb[:], in_=wf.rearrange("(p m) k -> p (m k)", m=M_TILES))
         for first, last in zip(load_starts[1:], load_ends[1:]):
@@ -95,7 +95,7 @@ def tile_afnb_pb_t_kernel(tc, context, high_feats, ww, bw, wf, bfuse, gf, bef, m
         def quantise(grouped, codes, scales):
             nc.vector.quantize_mx(out=codes.bitcast(FP8X4), scales=scales, in_=grouped)
 
-        def quantise_weight(w_sb, passes, name):
+        def transpose_weight(w_sb, passes, name):
             words = w_sb[:].bitcast(F32).rearrange("p (m g q u) -> p m g u q", m=M_TILES, g=passes, u=2)
             grouped = keep.tile([P, passes * M_TILES * P * PACK], BF16, align_bytes=64, name=name + "_grouped")
             pairs = grouped[:].bitcast(F32).rearrange("q (g m c u) -> q g m c u", g=passes, m=M_TILES, u=2)
@@ -106,6 +106,9 @@ def tile_afnb_pb_t_kernel(tc, context, high_feats, ww, bw, wf, bfuse, gf, bef, m
                         for u in range(2):
                             nc.tensor.transpose(bank[:, i, u, :], words[:, m0 + i, g, u, :], ident[:])
                     nc.scalar.copy(out=pairs[:, g, m0 : m0 + 2], in_=bank[:].rearrange("q i u c -> q i c u"))
+            return grouped
+
+        def quantise_weight(grouped, passes, name):
             codes = keep.tile([P, passes, M_TILES, P], U32, align_bytes=64, name=name + "_codes")
             scales = keep.tile([P, passes, M_TILES, P], U8, align_bytes=64, name=name + "_scales")
             quantise(
@@ -115,27 +118,43 @@ def tile_afnb_pb_t_kernel(tc, context, high_feats, ww, bw, wf, bfuse, gf, bef, m
             )
             return codes, scales
 
-        ctx_grouped, hi_grouped, c_grouped = {}, {}, {}
-        hi_codes, hi_scales, c_planes = {}, {}, {}
+        grouped_of = {}
+        codes_of = {}
+        c_planes = {}
 
-        def regroup_inputs(i):
+        def regroup_input(operand, raw, i):
+            if not 0 <= i < rounds:
+                return
             first, width = chunks[i]
             load = max(start for start in load_starts if start <= first)
-            col = first - load
-            ctx_grouped[i] = work.tile([P, CHUNK, PACK], BF16, align_bytes=64, name="ctx_grouped")
-            regroup(ctx_grouped[i][:, :width, :], ctx_raw[load][:, :, col : col + width])
-            hi_grouped[i] = work.tile([P, CHUNK, PACK], BF16, align_bytes=64, name="hi_grouped")
-            regroup(hi_grouped[i][:, :width, :], hi_raw[load][:, :, col : col + width])
+            grouped = work.tile([P, CHUNK, PACK], BF16, align_bytes=64, name=operand + "_grouped")
+            regroup(grouped[:, :width, :], raw[load][:, :, first - load : first - load + width])
+            grouped_of[operand, i] = grouped
+
+        def regroup_c(i):
+            if not 0 <= i < rounds:
+                return
+            width = chunks[i][1]
+            grouped = work.tile([P, CHUNK, PACK], BF16, align_bytes=64, name="c_grouped")
+            regroup(grouped[:, :width, :], c_planes[i][:, :, :width])
+            grouped_of["c", i] = grouped
+
+        def quantise_chunk(operand, i, bufs):
+            if not 0 <= i < rounds:
+                return
+            width = chunks[i][1]
+            codes = work.tile([P, CHUNK], U32, align_bytes=64, name=operand + "_codes", bufs=bufs)
+            scales = work.tile([P, CHUNK], U8, align_bytes=64, name=operand + "_scales", bufs=bufs)
+            quantise(
+                grouped_of[operand, i][:, :width, :].rearrange("p n t -> p (n t)"), codes[:, :width], scales[:, :width]
+            )
+            codes_of[operand, i] = (codes, scales)
 
         def first_product(i):
+            if not 0 <= i < rounds:
+                return
             width = chunks[i][1]
-            ctx_codes = work.tile([P, CHUNK], U32, align_bytes=64)
-            ctx_scales = work.tile([P, CHUNK], U8, align_bytes=64)
-            quantise(
-                ctx_grouped[i][:, :width, :].rearrange("p n t -> p (n t)"),
-                ctx_codes[:, :width],
-                ctx_scales[:, :width],
-            )
+            ctx_codes, ctx_scales = codes_of["ctx", i]
             c_planes[i] = work.tile([P, M_TILES, CHUNK], BF16, name="c_planes", bufs=LAG + 1)
             for m in range(M_TILES):
                 c_acc = psum.tile([P, CHUNK], F32)
@@ -151,52 +170,56 @@ def tile_afnb_pb_t_kernel(tc, context, high_feats, ww, bw, wf, bfuse, gf, bef, m
                 nc.scalar.activation(
                     out=c_planes[i][:, m, :width], in_=c_acc[:, :width], func=IDENTITY, bias=bw_f32[:, m : m + 1], scale=1.0
                 )
-            if i + 1 < rounds:
-                regroup_inputs(i + 1)
-            hi_codes[i] = work.tile([P, CHUNK], U32, align_bytes=64, name="hi_codes", bufs=LAG + 1)
-            hi_scales[i] = work.tile([P, CHUNK], U8, align_bytes=64, name="hi_scales", bufs=LAG + 1)
-            quantise(
-                hi_grouped[i][:, :width, :].rearrange("p n t -> p (n t)"),
-                hi_codes[i][:, :width],
-                hi_scales[i][:, :width],
-            )
-
-        def regroup_c(i):
-            width = chunks[i][1]
-            c_grouped[i] = work.tile([P, CHUNK, PACK], BF16, align_bytes=64, name="c_grouped")
-            regroup(c_grouped[i][:, :width, :], c_planes[i][:, :, :width])
 
         def second_product(i):
+            if not 0 <= i < rounds:
+                return
             first, width = chunks[i]
-            c_codes = work.tile([P, CHUNK], U32, align_bytes=64)
-            c_scales = work.tile([P, CHUNK], U8, align_bytes=64)
-            quantise(
-                c_grouped[i][:, :width, :].rearrange("p n t -> p (n t)"), c_codes[:, :width], c_scales[:, :width]
-            )
-            moving = [(c_codes, c_scales), (hi_codes[i], hi_scales[i])]
+            moving = [codes_of["c", i], codes_of["hi", i]]
+            vector_helps = i + LAG >= rounds
             y_sb = work.tile([P, M_TILES, CHUNK], F32, bufs=3)
             for m in range(M_TILES):
                 y_acc = psum.tile([P, CHUNK], F32)
-                for g in (1, 0):
+                for g in range(len(moving)):
                     nc.tensor.matmul_mx(
                         out=y_acc[:, :width],
                         lhsT=wf_codes[:, g, m, :].bitcast(FP8X4),
                         lhsT_scale=wf_scales[:, g, m, :],
                         rhs=moving[g][0][:, :width].bitcast(FP8X4),
                         rhs_scale=moving[g][1][:, :width],
-                        start=(g == 1),
-                        stop=(g == 0),
+                        start=(g == 0),
+                        stop=(g == len(moving) - 1),
                     )
-                nc.scalar.activation(
-                    out=y_sb[:, m, :width],
-                    in_=y_acc[:, :width],
-                    func=IDENTITY,
-                    scale=bn_scale[:, m : m + 1],
-                    bias=bn_shift[:, m : m + 1],
-                )
+                if vector_helps and m % 2 == 1:
+                    nc.vector.tensor_scalar(
+                        out=y_sb[:, m, :width],
+                        in0=y_acc[:, :width],
+                        scalar1=bn_scale[:, m : m + 1],
+                        scalar2=bn_shift[:, m : m + 1],
+                        op0=mybir.AluOpType.mult,
+                        op1=mybir.AluOpType.add,
+                    )
+                else:
+                    nc.scalar.activation(
+                        out=y_sb[:, m, :width],
+                        in_=y_acc[:, :width],
+                        func=IDENTITY,
+                        scale=bn_scale[:, m : m + 1],
+                        bias=bn_shift[:, m : m + 1],
+                    )
             for b, n0, n1 in batch_parts(first, first + width):
                 col = b * PIXELS + n0 - first
                 nc.sync.dma_start(out=out_rows[b, :, :, n0:n1], in_=y_sb[:, :, col : col + n1 - n0])
+
+        def one_round(i):
+            regroup_c(i - LAG)
+            quantise_chunk("ctx", i, 2)
+            first_product(i)
+            regroup_input("ctx", ctx_raw, i + 1)
+            quantise_chunk("c", i - LAG, 2)
+            second_product(i - LAG)
+            regroup_input("hi", hi_raw, i + 1)
+            quantise_chunk("hi", i, LAG + 1)
 
         bw_f32 = keep.tile([P, M_TILES], F32)
         nc.vector.tensor_copy(out=bw_f32[:], in_=bw_sb[:])
@@ -205,21 +228,18 @@ def tile_afnb_pb_t_kernel(tc, context, high_feats, ww, bw, wf, bfuse, gf, bef, m
         nc.vector.tensor_scalar_add(out=bn_scale[:], in0=vf_sb[:], scalar1=EPS)
         nc.scalar.sqrt(out=bn_scale[:], in_=bn_scale[:])
 
-        regroup_inputs(0)
-        ww_codes, ww_scales = quantise_weight(ww_sb, CV // K_PASS, "ww")
-        for i in range(LAG):
-            first_product(i)
+        ww_grouped = transpose_weight(ww_sb, CV // K_PASS, "ww")
+        wf_grouped = transpose_weight(wf_sb, (CO + CH) // K_PASS, "wf")
 
+        one_round(-1)
+        ww_codes, ww_scales = quantise_weight(ww_grouped, CV // K_PASS, "ww")
+        for i in range(LAG):
+            one_round(i)
         nc.vector.reciprocal(out=bn_scale[:], in_=bn_scale[:])
         nc.vector.tensor_mul(out=bn_scale[:], in0=bn_scale[:], in1=gf_sb[:])
         nc.vector.tensor_sub(out=bn_shift[:], in0=bfuse_sb[:], in1=mf_sb[:])
         nc.vector.tensor_mul(out=bn_shift[:], in0=bn_shift[:], in1=bn_scale[:])
         nc.vector.tensor_add(out=bn_shift[:], in0=bn_shift[:], in1=bef_sb[:])
-        wf_codes, wf_scales = quantise_weight(wf_sb, (CO + CH) // K_PASS, "wf")
-        for i in range(LAG, rounds):
-            regroup_c(i - LAG)
-            first_product(i)
-            second_product(i - LAG)
-        for i in range(rounds - LAG, rounds):
-            regroup_c(i)
-            second_product(i)
+        wf_codes, wf_scales = quantise_weight(wf_grouped, (CO + CH) // K_PASS, "wf")
+        for i in range(LAG, rounds + LAG):
+            one_round(i)

@@ -9,6 +9,8 @@ U32 = mybir.dt.uint32
 U8 = mybir.dt.uint8
 FP8X4 = mybir.dt.float8_e4m3fn_x4
 IDENTITY = mybir.ActivationFunctionType.Identity
+MULT = mybir.AluOpType.mult
+ADD = mybir.AluOpType.add
 
 P = 128
 PACK = 4
@@ -19,9 +21,9 @@ CV, CH, CO = 512, 512, 512
 COLS = BATCH * PIXELS
 CHUNK = 512
 M_TILES = CO // P
-LOAD_COLS = 2 * CHUNK
+BLOCK = 128
+MAX_LOAD = 4 * CHUNK
 RUN = 4
-LAG = 2
 EPS = 1e-5
 
 FLOPS = 2 * COLS * (CO * CV + CO * (CO + CH))
@@ -50,26 +52,27 @@ def tile_afnb_pb_t_kernel(tc, context, high_feats, ww, bw, wf, bfuse, gf, bef, m
         keep = stack.enter_context(tc.tile_pool(name="keep", bufs=1))
         work = stack.enter_context(tc.tile_pool(name="work", bufs=2))
         psum = stack.enter_context(tc.psum_pool(name="psum", bufs=4))
+        stack.enter_context(tc.manual_schedule())
 
         ww_sb = keep.tile([P, M_TILES * CV], BF16)
         wf_sb = keep.tile([P, M_TILES * (CO + CH)], BF16)
-        ctx_raw, hi_raw = {}, {}
-
-        def load_columns(raw, rows, name, first, last):
-            raw[first] = keep.tile([P, PACK, last - first], BF16, name="%s_%d" % (name, first))
-            for b, n0, n1 in batch_parts(first, last):
-                col = b * PIXELS + n0 - first
-                nc.sync.dma_start(out=raw[first][:, :, col : col + n1 - n0], in_=rows[b, :, :, n0:n1])
-
-        load_starts = [0] + list(range(CHUNK, COLS, LOAD_COLS))
-        load_ends = load_starts[1:] + [COLS]
-        load_columns(ctx_raw, ctx_rows, "ctx_raw", load_starts[0], load_ends[0])
         nc.sync.dma_start(out=ww_sb[:], in_=ww.rearrange("(p m) k -> p (m k)", m=M_TILES))
-        load_columns(hi_raw, hi_rows, "hi_raw", load_starts[0], load_ends[0])
-        nc.sync.dma_start(out=wf_sb[:], in_=wf.rearrange("(p m) k -> p (m k)", m=M_TILES))
-        for first, last in zip(load_starts[1:], load_ends[1:]):
-            load_columns(ctx_raw, ctx_rows, "ctx_raw", first, last)
-            load_columns(hi_raw, hi_rows, "hi_raw", first, last)
+
+        load_starts = []
+        first, load_width = 0, CHUNK
+        while first < COLS:
+            load_starts.append(first)
+            first += load_width
+            load_width = min(2 * load_width, MAX_LOAD)
+        ctx_raw, hi_raw = {}, {}
+        for first, last in zip(load_starts, load_starts[1:] + [COLS]):
+            for raw, rows, name in ((hi_raw, hi_rows, "hi_raw"), (ctx_raw, ctx_rows, "ctx_raw")):
+                raw[first] = keep.tile([P, PACK, last - first], BF16, name="%s_%d" % (name, first))
+                for b, n0, n1 in batch_parts(first, last):
+                    col = b * PIXELS + n0 - first
+                    nc.sync.dma_start(out=raw[first][:, :, col : col + n1 - n0], in_=rows[b, :, :, n0:n1])
+            if first == load_starts[1]:
+                nc.sync.dma_start(out=wf_sb[:], in_=wf.rearrange("(p m) k -> p (m k)", m=M_TILES))
 
         def load_vector(vec, name):
             vec_sb = keep.tile([P, M_TILES], BF16, name=name)
@@ -85,15 +88,6 @@ def tile_afnb_pb_t_kernel(tc, context, high_feats, ww, bw, wf, bfuse, gf, bef, m
 
         ident = keep.tile([P, P], F32)
         make_identity(nc, ident[:])
-
-        def regroup(grouped, planes):
-            nc.vector.tensor_copy(
-                out=grouped.rearrange("p (c i) t -> p c t i", i=RUN),
-                in_=planes.rearrange("p t (c i) -> p c t i", i=RUN),
-            )
-
-        def quantise(grouped, codes, scales):
-            nc.vector.quantize_mx(out=codes.bitcast(FP8X4), scales=scales, in_=grouped)
 
         def transpose_weight(w_sb, passes, name):
             words = w_sb[:].bitcast(F32).rearrange("p (m g q u) -> p m g u q", m=M_TILES, g=passes, u=2)
@@ -111,33 +105,54 @@ def tile_afnb_pb_t_kernel(tc, context, high_feats, ww, bw, wf, bfuse, gf, bef, m
         def quantise_weight(grouped, passes, name):
             codes = keep.tile([P, passes, M_TILES, P], U32, align_bytes=64, name=name + "_codes")
             scales = keep.tile([P, passes, M_TILES, P], U8, align_bytes=64, name=name + "_scales")
-            quantise(
-                grouped[:],
-                codes[:].rearrange("q g m c -> q (g m c)"),
-                scales[:].rearrange("q g m c -> q (g m c)"),
+            nc.vector.quantize_mx(
+                out=codes[:].rearrange("q g m c -> q (g m c)").bitcast(FP8X4),
+                scales=scales[:].rearrange("q g m c -> q (g m c)"),
+                in_=grouped[:],
             )
             return codes, scales
 
         grouped_of = {}
         codes_of = {}
-        c_planes = {}
+        c_banks = {}
 
-        def regroup_input(operand, raw, i):
-            if not 0 <= i < rounds:
-                return
-            first, width = chunks[i]
+        def raw_columns(raw, i, lo, hi):
+            first = chunks[i][0]
             load = max(start for start in load_starts if start <= first)
-            grouped = work.tile([P, CHUNK, PACK], BF16, align_bytes=64, name=operand + "_grouped")
-            regroup(grouped[:, :width, :], raw[load][:, :, first - load : first - load + width])
-            grouped_of[operand, i] = grouped
+            return raw[load][:, :, first - load + lo : first - load + hi]
 
-        def regroup_c(i):
+        def by_runs(grouped, planes):
+            return (
+                grouped.rearrange("p (c i) t -> p c t i", i=RUN),
+                planes.rearrange("p t (c i) -> p c t i", i=RUN),
+            )
+
+        def regroup_ctx(i):
             if not 0 <= i < rounds:
                 return
             width = chunks[i][1]
-            grouped = work.tile([P, CHUNK, PACK], BF16, align_bytes=64, name="c_grouped")
-            regroup(grouped[:, :width, :], c_planes[i][:, :, :width])
-            grouped_of["c", i] = grouped
+            grouped = work.tile([P, CHUNK, PACK], BF16, align_bytes=64, name="ctx_grouped", bufs=3)
+            dst, src = by_runs(grouped[:, :width, :], raw_columns(ctx_raw, i, 0, width))
+            nc.scalar.copy(out=dst, in_=src)
+            grouped_of["ctx", i] = grouped
+
+        def regroup_hi(i):
+            if not 0 <= i < rounds:
+                return
+            width = chunks[i][1]
+            split = width * 3 // 4
+            grouped = work.tile([P, CHUNK, PACK], BF16, align_bytes=64, name="hi_grouped", bufs=1)
+            nc.gpsimd.tensor_scalar(
+                out=grouped[:, :split, :],
+                in0=raw_columns(hi_raw, i, 0, split).rearrange("p t n -> p n t"),
+                scalar1=1.0,
+                scalar2=0.0,
+                op0=MULT,
+                op1=ADD,
+            )
+            dst, src = by_runs(grouped[:, split:width, :], raw_columns(hi_raw, i, split, width))
+            nc.vector.tensor_copy(out=dst, in_=src)
+            grouped_of["hi", i] = grouped
 
         def quantise_chunk(operand, i, bufs):
             if not 0 <= i < rounds:
@@ -145,8 +160,10 @@ def tile_afnb_pb_t_kernel(tc, context, high_feats, ww, bw, wf, bfuse, gf, bef, m
             width = chunks[i][1]
             codes = work.tile([P, CHUNK], U32, align_bytes=64, name=operand + "_codes", bufs=bufs)
             scales = work.tile([P, CHUNK], U8, align_bytes=64, name=operand + "_scales", bufs=bufs)
-            quantise(
-                grouped_of[operand, i][:, :width, :].rearrange("p n t -> p (n t)"), codes[:, :width], scales[:, :width]
+            nc.vector.quantize_mx(
+                out=codes[:, :width].bitcast(FP8X4),
+                scales=scales[:, :width],
+                in_=grouped_of[operand, i][:, :width, :].rearrange("p n t -> p (n t)"),
             )
             codes_of[operand, i] = (codes, scales)
 
@@ -155,29 +172,40 @@ def tile_afnb_pb_t_kernel(tc, context, high_feats, ww, bw, wf, bfuse, gf, bef, m
                 return
             width = chunks[i][1]
             ctx_codes, ctx_scales = codes_of["ctx", i]
-            c_planes[i] = work.tile([P, M_TILES, CHUNK], BF16, name="c_planes", bufs=LAG + 1)
-            for m in range(M_TILES):
-                c_acc = psum.tile([P, CHUNK], F32)
-                nc.tensor.matmul_mx(
-                    out=c_acc[:, :width],
-                    lhsT=ww_codes[:, 0, m, :].bitcast(FP8X4),
-                    lhsT_scale=ww_scales[:, 0, m, :],
-                    rhs=ctx_codes[:, :width].bitcast(FP8X4),
-                    rhs_scale=ctx_scales[:, :width],
-                    start=True,
-                    stop=True,
+            c_banks[i] = []
+            for n0 in range(0, width, BLOCK):
+                bank = psum.tile([P, M_TILES, BLOCK], F32, name="c_acc")
+                for m in range(M_TILES):
+                    nc.tensor.matmul_mx(
+                        out=bank[:, m, :],
+                        lhsT=ww_codes[:, 0, m, :].bitcast(FP8X4),
+                        lhsT_scale=ww_scales[:, 0, m, :],
+                        rhs=ctx_codes[:, n0 : n0 + BLOCK].bitcast(FP8X4),
+                        rhs_scale=ctx_scales[:, n0 : n0 + BLOCK],
+                        start=True,
+                        stop=True,
+                    )
+                c_banks[i].append(bank)
+
+        def drain_c(i):
+            if not 0 <= i < rounds:
+                return
+            grouped = work.tile([P, CHUNK, PACK], BF16, align_bytes=64, name="c_grouped")
+            for k, bank in enumerate(c_banks[i]):
+                nc.vector.tensor_tensor(
+                    out=grouped[:, k * BLOCK : (k + 1) * BLOCK, :],
+                    in0=bank[:].rearrange("p m n -> p n m"),
+                    in1=bw_f32[:].unsqueeze(1).to_broadcast([P, BLOCK, M_TILES]),
+                    op=ADD,
                 )
-                nc.scalar.activation(
-                    out=c_planes[i][:, m, :width], in_=c_acc[:, :width], func=IDENTITY, bias=bw_f32[:, m : m + 1], scale=1.0
-                )
+            grouped_of["c", i] = grouped
 
         def second_product(i):
             if not 0 <= i < rounds:
                 return
             first, width = chunks[i]
             moving = [codes_of["c", i], codes_of["hi", i]]
-            vector_helps = i + LAG >= rounds
-            y_sb = work.tile([P, M_TILES, CHUNK], F32, bufs=3)
+            y_sb = work.tile([P, M_TILES, CHUNK], F32, bufs=5)
             for m in range(M_TILES):
                 y_acc = psum.tile([P, CHUNK], F32)
                 for g in range(len(moving)):
@@ -190,36 +218,16 @@ def tile_afnb_pb_t_kernel(tc, context, high_feats, ww, bw, wf, bfuse, gf, bef, m
                         start=(g == 0),
                         stop=(g == len(moving) - 1),
                     )
-                if vector_helps and m % 2 == 1:
-                    nc.vector.tensor_scalar(
-                        out=y_sb[:, m, :width],
-                        in0=y_acc[:, :width],
-                        scalar1=bn_scale[:, m : m + 1],
-                        scalar2=bn_shift[:, m : m + 1],
-                        op0=mybir.AluOpType.mult,
-                        op1=mybir.AluOpType.add,
-                    )
-                else:
-                    nc.scalar.activation(
-                        out=y_sb[:, m, :width],
-                        in_=y_acc[:, :width],
-                        func=IDENTITY,
-                        scale=bn_scale[:, m : m + 1],
-                        bias=bn_shift[:, m : m + 1],
-                    )
+                nc.scalar.activation(
+                    out=y_sb[:, m, :width],
+                    in_=y_acc[:, :width],
+                    func=IDENTITY,
+                    scale=bn_scale[:, m : m + 1],
+                    bias=bn_shift[:, m : m + 1],
+                )
             for b, n0, n1 in batch_parts(first, first + width):
                 col = b * PIXELS + n0 - first
                 nc.sync.dma_start(out=out_rows[b, :, :, n0:n1], in_=y_sb[:, :, col : col + n1 - n0])
-
-        def one_round(i):
-            regroup_c(i - LAG)
-            quantise_chunk("ctx", i, 2)
-            first_product(i)
-            regroup_input("ctx", ctx_raw, i + 1)
-            quantise_chunk("c", i - LAG, 2)
-            second_product(i - LAG)
-            regroup_input("hi", hi_raw, i + 1)
-            quantise_chunk("hi", i, LAG + 1)
 
         bw_f32 = keep.tile([P, M_TILES], F32)
         nc.vector.tensor_copy(out=bw_f32[:], in_=bw_sb[:])
@@ -228,18 +236,27 @@ def tile_afnb_pb_t_kernel(tc, context, high_feats, ww, bw, wf, bfuse, gf, bef, m
         nc.vector.tensor_scalar_add(out=bn_scale[:], in0=vf_sb[:], scalar1=EPS)
         nc.scalar.sqrt(out=bn_scale[:], in_=bn_scale[:])
 
-        ww_grouped = transpose_weight(ww_sb, CV // K_PASS, "ww")
-        wf_grouped = transpose_weight(wf_sb, (CO + CH) // K_PASS, "wf")
+        def one_round(i):
+            drain_c(i)
+            second_product(i - 1)
+            regroup_hi(i + 1)
+            quantise_chunk("ctx", i + 1, 2)
+            first_product(i + 1)
+            quantise_chunk("c", i, 2)
+            quantise_chunk("hi", i + 1, 3)
+            regroup_ctx(i + 2)
 
-        one_round(-1)
+        ww_grouped = transpose_weight(ww_sb, CV // K_PASS, "ww")
         ww_codes, ww_scales = quantise_weight(ww_grouped, CV // K_PASS, "ww")
-        for i in range(LAG):
-            one_round(i)
+        regroup_ctx(0)
+        one_round(-1)
+        wf_grouped = transpose_weight(wf_sb, (CO + CH) // K_PASS, "wf")
+        one_round(0)
         nc.vector.reciprocal(out=bn_scale[:], in_=bn_scale[:])
         nc.vector.tensor_mul(out=bn_scale[:], in0=bn_scale[:], in1=gf_sb[:])
         nc.vector.tensor_sub(out=bn_shift[:], in0=bfuse_sb[:], in1=mf_sb[:])
         nc.vector.tensor_mul(out=bn_shift[:], in0=bn_shift[:], in1=bn_scale[:])
         nc.vector.tensor_add(out=bn_shift[:], in0=bn_shift[:], in1=bef_sb[:])
         wf_codes, wf_scales = quantise_weight(wf_grouped, (CO + CH) // K_PASS, "wf")
-        for i in range(LAG, rounds + LAG):
+        for i in range(1, rounds + 1):
             one_round(i)

@@ -66,7 +66,7 @@ def tile_afnb_pb_t_kernel(tc, context, high_feats, ww, bw, wf, bfuse, gf, bef, m
             load_width = min(2 * load_width, MAX_LOAD)
         ctx_raw, hi_raw = {}, {}
         for first, last in zip(load_starts, load_starts[1:] + [COLS]):
-            for raw, rows, name in ((hi_raw, hi_rows, "hi_raw"), (ctx_raw, ctx_rows, "ctx_raw")):
+            for raw, rows, name in ((ctx_raw, ctx_rows, "ctx_raw"), (hi_raw, hi_rows, "hi_raw")):
                 raw[first] = keep.tile([P, PACK, last - first], BF16, name="%s_%d" % (name, first))
                 for b, n0, n1 in batch_parts(first, last):
                     col = b * PIXELS + n0 - first
@@ -205,7 +205,8 @@ def tile_afnb_pb_t_kernel(tc, context, high_feats, ww, bw, wf, bfuse, gf, bef, m
                 return
             first, width = chunks[i]
             moving = [codes_of["c", i], codes_of["hi", i]]
-            y_sb = work.tile([P, M_TILES, CHUNK], F32, bufs=5)
+            vector_helps = i == rounds - 1
+            y_sb = work.tile([P, M_TILES, CHUNK], F32, bufs=6)
             for m in range(M_TILES):
                 y_acc = psum.tile([P, CHUNK], F32)
                 for g in range(len(moving)):
@@ -218,13 +219,23 @@ def tile_afnb_pb_t_kernel(tc, context, high_feats, ww, bw, wf, bfuse, gf, bef, m
                         start=(g == 0),
                         stop=(g == len(moving) - 1),
                     )
-                nc.scalar.activation(
-                    out=y_sb[:, m, :width],
-                    in_=y_acc[:, :width],
-                    func=IDENTITY,
-                    scale=bn_scale[:, m : m + 1],
-                    bias=bn_shift[:, m : m + 1],
-                )
+                if vector_helps and m % 2 == 1:
+                    nc.vector.tensor_scalar(
+                        out=y_sb[:, m, :width],
+                        in0=y_acc[:, :width],
+                        scalar1=bn_scale[:, m : m + 1],
+                        scalar2=bn_shift[:, m : m + 1],
+                        op0=MULT,
+                        op1=ADD,
+                    )
+                else:
+                    nc.scalar.activation(
+                        out=y_sb[:, m, :width],
+                        in_=y_acc[:, :width],
+                        func=IDENTITY,
+                        scale=bn_scale[:, m : m + 1],
+                        bias=bn_shift[:, m : m + 1],
+                    )
             for b, n0, n1 in batch_parts(first, first + width):
                 col = b * PIXELS + n0 - first
                 nc.sync.dma_start(out=out_rows[b, :, :, n0:n1], in_=y_sb[:, :, col : col + n1 - n0])

@@ -54,12 +54,21 @@ def tile_afnb_pb_t_kernel(tc, context, high_feats, ww, bw, wf, bfuse, gf, bef, m
         psum = stack.enter_context(tc.psum_pool(name="psum", bufs=4))
         stack.enter_context(tc.manual_schedule())
 
+        warm = keep.tile([P, 1], F32)
+        nc.vector.memset(warm[:], 1.0)
+        nc.scalar.sqrt(out=warm[:], in_=warm[:])
+
+        def load_vector(vec, name):
+            vec_sb = keep.tile([P, M_TILES], BF16, name=name)
+            nc.sync.dma_start(out=vec_sb[:], in_=vec.rearrange("(p m) -> p m", m=M_TILES))
+            return vec_sb
+
         ww_sb = keep.tile([P, M_TILES * CV], BF16)
         wf_sb = keep.tile([P, M_TILES * (CO + CH)], BF16)
         nc.sync.dma_start(out=ww_sb[:], in_=ww.rearrange("(p m) k -> p (m k)", m=M_TILES))
 
-        load_starts = []
-        first, load_width = 0, CHUNK
+        load_starts = [0]
+        first, load_width = CHUNK, CHUNK
         while first < COLS:
             load_starts.append(first)
             first += load_width
@@ -71,25 +80,20 @@ def tile_afnb_pb_t_kernel(tc, context, high_feats, ww, bw, wf, bfuse, gf, bef, m
                 for b, n0, n1 in batch_parts(first, last):
                     col = b * PIXELS + n0 - first
                     nc.sync.dma_start(out=raw[first][:, :, col : col + n1 - n0], in_=rows[b, :, :, n0:n1])
-            if first == load_starts[1]:
-                nc.sync.dma_start(out=wf_sb[:], in_=wf.rearrange("(p m) k -> p (m k)", m=M_TILES))
-
-        def load_vector(vec, name):
-            vec_sb = keep.tile([P, M_TILES], BF16, name=name)
-            nc.scalar.dma_start(out=vec_sb[:], in_=vec.rearrange("(p m) -> p m", m=M_TILES))
-            return vec_sb
-
-        bw_sb = load_vector(bw, "bw_sb")
-        vf_sb = load_vector(vf, "vf_sb")
-        gf_sb = load_vector(gf, "gf_sb")
-        bfuse_sb = load_vector(bfuse, "bfuse_sb")
-        mf_sb = load_vector(mf, "mf_sb")
-        bef_sb = load_vector(bef, "bef_sb")
+                if first == load_starts[0] and name == "ctx_raw":
+                    bw_sb = load_vector(bw, "bw_sb")
+                    vf_sb = load_vector(vf, "vf_sb")
+                if first == load_starts[1] and name == "ctx_raw":
+                    nc.sync.dma_start(out=wf_sb[:], in_=wf.rearrange("(p m) k -> p (m k)", m=M_TILES))
+                    gf_sb = load_vector(gf, "gf_sb")
+                    bfuse_sb = load_vector(bfuse, "bfuse_sb")
+                    mf_sb = load_vector(mf, "mf_sb")
+                    bef_sb = load_vector(bef, "bef_sb")
 
         ident = keep.tile([P, P], F32)
         make_identity(nc, ident[:])
 
-        def transpose_weight(w_sb, passes, name):
+        def transpose_weight(w_sb, passes, name, copy_out):
             words = w_sb[:].bitcast(F32).rearrange("p (m g q u) -> p m g u q", m=M_TILES, g=passes, u=2)
             grouped = keep.tile([P, passes * M_TILES * P * PACK], BF16, align_bytes=64, name=name + "_grouped")
             pairs = grouped[:].bitcast(F32).rearrange("q (g m c u) -> q g m c u", g=passes, m=M_TILES, u=2)
@@ -99,7 +103,7 @@ def tile_afnb_pb_t_kernel(tc, context, high_feats, ww, bw, wf, bfuse, gf, bef, m
                     for i in range(2):
                         for u in range(2):
                             nc.tensor.transpose(bank[:, i, u, :], words[:, m0 + i, g, u, :], ident[:])
-                    nc.scalar.copy(out=pairs[:, g, m0 : m0 + 2], in_=bank[:].rearrange("q i u c -> q i c u"))
+                    copy_out(out=pairs[:, g, m0 : m0 + 2], in_=bank[:].rearrange("q i u c -> q i c u"))
             return grouped
 
         def quantise_weight(grouped, passes, name):
@@ -241,11 +245,8 @@ def tile_afnb_pb_t_kernel(tc, context, high_feats, ww, bw, wf, bfuse, gf, bef, m
                 nc.sync.dma_start(out=out_rows[b, :, :, n0:n1], in_=y_sb[:, :, col : col + n1 - n0])
 
         bw_f32 = keep.tile([P, M_TILES], F32)
-        nc.vector.tensor_copy(out=bw_f32[:], in_=bw_sb[:])
         bn_scale = keep.tile([P, M_TILES], F32)
         bn_shift = keep.tile([P, M_TILES], F32)
-        nc.vector.tensor_scalar_add(out=bn_scale[:], in0=vf_sb[:], scalar1=EPS)
-        nc.scalar.sqrt(out=bn_scale[:], in_=bn_scale[:])
 
         def one_round(i):
             drain_c(i)
@@ -257,11 +258,14 @@ def tile_afnb_pb_t_kernel(tc, context, high_feats, ww, bw, wf, bfuse, gf, bef, m
             quantise_chunk("hi", i + 1, 3)
             regroup_ctx(i + 2)
 
-        ww_grouped = transpose_weight(ww_sb, CV // K_PASS, "ww")
+        ww_grouped = transpose_weight(ww_sb, CV // K_PASS, "ww", nc.vector.tensor_copy)
         ww_codes, ww_scales = quantise_weight(ww_grouped, CV // K_PASS, "ww")
         regroup_ctx(0)
         one_round(-1)
-        wf_grouped = transpose_weight(wf_sb, (CO + CH) // K_PASS, "wf")
+        nc.vector.tensor_copy(out=bw_f32[:], in_=bw_sb[:])
+        nc.vector.tensor_scalar_add(out=bn_scale[:], in0=vf_sb[:], scalar1=EPS)
+        nc.scalar.sqrt(out=bn_scale[:], in_=bn_scale[:])
+        wf_grouped = transpose_weight(wf_sb, (CO + CH) // K_PASS, "wf", nc.scalar.copy)
         one_round(0)
         nc.vector.reciprocal(out=bn_scale[:], in_=bn_scale[:])
         nc.vector.tensor_mul(out=bn_scale[:], in0=bn_scale[:], in1=gf_sb[:])

@@ -74,21 +74,26 @@ def tile_afnb_pb_t_kernel(tc, context, high_feats, ww, bw, wf, bfuse, gf, bef, m
             first += load_width
             load_width = min(2 * load_width, MAX_LOAD)
         ctx_raw, hi_raw = {}, {}
+        wanted = [(0, 1, "wf", 0, 0)]
         for first, last in zip(load_starts, load_starts[1:] + [COLS]):
-            for raw, rows, name in ((ctx_raw, ctx_rows, "ctx_raw"), (hi_raw, hi_rows, "hi_raw")):
+            wanted.append((first // CHUNK - 2, 2, "ctx_raw", first, last))
+            wanted.append((first // CHUNK, 0, "hi_raw", first, last))
+        for need, rank, name, first, last in sorted(wanted):
+            if name == "wf":
+                nc.sync.dma_start(out=wf_sb[:], in_=wf.rearrange("(p m) k -> p (m k)", m=M_TILES))
+                gf_sb = load_vector(gf, "gf_sb")
+                bfuse_sb = load_vector(bfuse, "bfuse_sb")
+                mf_sb = load_vector(mf, "mf_sb")
+                bef_sb = load_vector(bef, "bef_sb")
+            else:
+                raw, rows = (ctx_raw, ctx_rows) if name == "ctx_raw" else (hi_raw, hi_rows)
                 raw[first] = keep.tile([P, PACK, last - first], BF16, name="%s_%d" % (name, first))
                 for b, n0, n1 in batch_parts(first, last):
                     col = b * PIXELS + n0 - first
                     nc.sync.dma_start(out=raw[first][:, :, col : col + n1 - n0], in_=rows[b, :, :, n0:n1])
-                if first == load_starts[0] and name == "ctx_raw":
+                if first == 0 and name == "ctx_raw":
                     bw_sb = load_vector(bw, "bw_sb")
                     vf_sb = load_vector(vf, "vf_sb")
-                if first == load_starts[1] and name == "ctx_raw":
-                    nc.sync.dma_start(out=wf_sb[:], in_=wf.rearrange("(p m) k -> p (m k)", m=M_TILES))
-                    gf_sb = load_vector(gf, "gf_sb")
-                    bfuse_sb = load_vector(bfuse, "bfuse_sb")
-                    mf_sb = load_vector(mf, "mf_sb")
-                    bef_sb = load_vector(bef, "bef_sb")
 
         ident = keep.tile([P, P], F32)
         make_identity(nc, ident[:])
@@ -140,12 +145,14 @@ def tile_afnb_pb_t_kernel(tc, context, high_feats, ww, bw, wf, bfuse, gf, bef, m
             nc.scalar.copy(out=dst, in_=src)
             grouped_of["ctx", i] = grouped
 
-        def regroup_hi(i):
+        def regroup_hi_gpsimd(i):
             if not 0 <= i < rounds:
                 return
             width = chunks[i][1]
             split = width * 3 // 4
             grouped = work.tile([P, CHUNK, PACK], BF16, align_bytes=64, name="hi_grouped", bufs=1)
+            if i == 0:
+                nc.vector.memset(grouped[:, 0:1, :], 0.0)
             nc.gpsimd.tensor_scalar(
                 out=grouped[:, :split, :],
                 in0=raw_columns(hi_raw, i, 0, split).rearrange("p t n -> p n t"),
@@ -154,8 +161,21 @@ def tile_afnb_pb_t_kernel(tc, context, high_feats, ww, bw, wf, bfuse, gf, bef, m
                 op0=MULT,
                 op1=ADD,
             )
-            dst, src = by_runs(grouped[:, split:width, :], raw_columns(hi_raw, i, split, width))
+            grouped_of["hi", i] = grouped
+
+        def regroup_hi_vector(i):
+            if not 0 <= i < rounds:
+                return
+            width = chunks[i][1]
+            split = width * 3 // 4
+            dst, src = by_runs(grouped_of["hi", i][:, split:width, :], raw_columns(hi_raw, i, split, width))
             nc.vector.tensor_copy(out=dst, in_=src)
+
+        def regroup_hi_scalar(i):
+            width = chunks[i][1]
+            grouped = work.tile([P, CHUNK, PACK], BF16, align_bytes=64, name="ctx_grouped", bufs=3)
+            dst, src = by_runs(grouped[:, :width, :], raw_columns(hi_raw, i, 0, width))
+            nc.scalar.copy(out=dst, in_=src)
             grouped_of["hi", i] = grouped
 
         def quantise_chunk(operand, i, bufs):
@@ -249,14 +269,21 @@ def tile_afnb_pb_t_kernel(tc, context, high_feats, ww, bw, wf, bfuse, gf, bef, m
         bn_shift = keep.tile([P, M_TILES], F32)
 
         def one_round(i):
+            if i < rounds - 1:
+                regroup_hi_gpsimd(i)
             drain_c(i)
             second_product(i - 1)
-            regroup_hi(i + 1)
+            if i < rounds - 1:
+                regroup_hi_vector(i)
             quantise_chunk("ctx", i + 1, 2)
             first_product(i + 1)
             quantise_chunk("c", i, 2)
-            quantise_chunk("hi", i + 1, 3)
+            if i < rounds - 1:
+                quantise_chunk("hi", i, 2)
             regroup_ctx(i + 2)
+            if i == rounds - 2:
+                regroup_hi_scalar(i + 1)
+                quantise_chunk("hi", i + 1, 2)
 
         ww_grouped = transpose_weight(ww_sb, CV // K_PASS, "ww", nc.vector.tensor_copy)
         ww_codes, ww_scales = quantise_weight(ww_grouped, CV // K_PASS, "ww")

@@ -111,15 +111,17 @@ def tile_afnb_pb_t_kernel(tc, context, high_feats, ww, bw, wf, bfuse, gf, bef, m
                     copy_out(out=pairs[:, g, m0 : m0 + 2], in_=bank[:].rearrange("q i u c -> q i c u"))
             return grouped
 
-        def quantise_weight(grouped, passes, name):
+        def weight_tiles(passes, name):
             codes = keep.tile([P, passes, M_TILES, P], U32, align_bytes=64, name=name + "_codes")
             scales = keep.tile([P, passes, M_TILES, P], U8, align_bytes=64, name=name + "_scales")
+            return codes, scales
+
+        def quantise_weight(grouped, codes, scales):
             nc.vector.quantize_mx(
                 out=codes[:].rearrange("q g m c -> q (g m c)").bitcast(FP8X4),
                 scales=scales[:].rearrange("q g m c -> q (g m c)"),
                 in_=grouped[:],
             )
-            return codes, scales
 
         grouped_of = {}
         codes_of = {}
@@ -268,6 +270,14 @@ def tile_afnb_pb_t_kernel(tc, context, high_feats, ww, bw, wf, bfuse, gf, bef, m
         bn_scale = keep.tile([P, M_TILES], F32)
         bn_shift = keep.tile([P, M_TILES], F32)
 
+        def prepare_second_product():
+            nc.vector.reciprocal(out=bn_scale[:], in_=bn_scale[:])
+            nc.vector.tensor_mul(out=bn_scale[:], in0=bn_scale[:], in1=gf_sb[:])
+            nc.vector.tensor_sub(out=bn_shift[:], in0=bfuse_sb[:], in1=mf_sb[:])
+            nc.vector.tensor_mul(out=bn_shift[:], in0=bn_shift[:], in1=bn_scale[:])
+            nc.vector.tensor_add(out=bn_shift[:], in0=bn_shift[:], in1=bef_sb[:])
+            quantise_weight(wf_grouped, wf_codes, wf_scales)
+
         def one_round(i):
             if i < rounds - 1:
                 regroup_hi_gpsimd(i)
@@ -278,6 +288,8 @@ def tile_afnb_pb_t_kernel(tc, context, high_feats, ww, bw, wf, bfuse, gf, bef, m
             quantise_chunk("ctx", i + 1, 2)
             first_product(i + 1)
             quantise_chunk("c", i, 2)
+            if i == 0:
+                prepare_second_product()
             if i < rounds - 1:
                 quantise_chunk("hi", i, 2)
             regroup_ctx(i + 2)
@@ -286,19 +298,14 @@ def tile_afnb_pb_t_kernel(tc, context, high_feats, ww, bw, wf, bfuse, gf, bef, m
                 quantise_chunk("hi", i + 1, 2)
 
         ww_grouped = transpose_weight(ww_sb, CV // K_PASS, "ww", nc.vector.tensor_copy)
-        ww_codes, ww_scales = quantise_weight(ww_grouped, CV // K_PASS, "ww")
+        ww_codes, ww_scales = weight_tiles(CV // K_PASS, "ww")
+        wf_codes, wf_scales = weight_tiles((CO + CH) // K_PASS, "wf")
+        quantise_weight(ww_grouped, ww_codes, ww_scales)
         regroup_ctx(0)
         one_round(-1)
         nc.vector.tensor_copy(out=bw_f32[:], in_=bw_sb[:])
         nc.vector.tensor_scalar_add(out=bn_scale[:], in0=vf_sb[:], scalar1=EPS)
         nc.scalar.sqrt(out=bn_scale[:], in_=bn_scale[:])
         wf_grouped = transpose_weight(wf_sb, (CO + CH) // K_PASS, "wf", nc.scalar.copy)
-        one_round(0)
-        nc.vector.reciprocal(out=bn_scale[:], in_=bn_scale[:])
-        nc.vector.tensor_mul(out=bn_scale[:], in0=bn_scale[:], in1=gf_sb[:])
-        nc.vector.tensor_sub(out=bn_shift[:], in0=bfuse_sb[:], in1=mf_sb[:])
-        nc.vector.tensor_mul(out=bn_shift[:], in0=bn_shift[:], in1=bn_scale[:])
-        nc.vector.tensor_add(out=bn_shift[:], in0=bn_shift[:], in1=bef_sb[:])
-        wf_codes, wf_scales = quantise_weight(wf_grouped, (CO + CH) // K_PASS, "wf")
-        for i in range(1, rounds + 1):
+        for i in range(rounds + 1):
             one_round(i)

@@ -24,6 +24,8 @@ M_TILES = CO // P
 BLOCK = 128
 MAX_LOAD = 4 * CHUNK
 RUN = 4
+SPIN_FIRST = 6
+SPIN_NEXT = 8
 EPS = 1e-5
 
 FLOPS = 2 * COLS * (CO * CV + CO * (CO + CH))
@@ -98,6 +100,16 @@ def tile_afnb_pb_t_kernel(tc, context, high_feats, ww, bw, wf, bfuse, gf, bef, m
         ident = keep.tile([P, P], F32)
         make_identity(nc, ident[:])
 
+        zeros = keep.tile([P, CHUNK], BF16)
+        nc.vector.memset(zeros[:], 0.0)
+
+        def spin(count):
+            idle = psum.tile([P, CHUNK], F32, name="idle", tag="c_acc")
+            for k in range(count):
+                nc.tensor.matmul(out=idle[:], lhsT=zeros[:, :P], rhs=zeros[:], start=True, stop=True)
+
+        spin(SPIN_FIRST)
+
         def transpose_weight(w_sb, passes, name, copy_out):
             words = w_sb[:].bitcast(F32).rearrange("p (m g q u) -> p m g u q", m=M_TILES, g=passes, u=2)
             grouped = keep.tile([P, passes * M_TILES * P * PACK], BF16, align_bytes=64, name=name + "_grouped")
@@ -143,8 +155,18 @@ def tile_afnb_pb_t_kernel(tc, context, high_feats, ww, bw, wf, bfuse, gf, bef, m
                 return
             width = chunks[i][1]
             grouped = work.tile([P, CHUNK, PACK], BF16, align_bytes=64, name="ctx_grouped", bufs=3)
-            dst, src = by_runs(grouped[:, :width, :], raw_columns(ctx_raw, i, 0, width))
+            split = width * 5 // 8 if i == 0 else width
+            dst, src = by_runs(grouped[:, :split, :], raw_columns(ctx_raw, i, 0, split))
             nc.scalar.copy(out=dst, in_=src)
+            if split < width:
+                nc.gpsimd.tensor_scalar(
+                    out=grouped[:, split:width, :],
+                    in0=raw_columns(ctx_raw, i, split, width).rearrange("p t n -> p n t"),
+                    scalar1=1.0,
+                    scalar2=0.0,
+                    op0=MULT,
+                    op1=ADD,
+                )
             grouped_of["ctx", i] = grouped
 
         def regroup_hi_gpsimd(i):
@@ -262,9 +284,14 @@ def tile_afnb_pb_t_kernel(tc, context, high_feats, ww, bw, wf, bfuse, gf, bef, m
                         scale=bn_scale[:, m : m + 1],
                         bias=bn_shift[:, m : m + 1],
                     )
-            for b, n0, n1 in batch_parts(first, first + width):
-                col = b * PIXELS + n0 - first
-                nc.sync.dma_start(out=out_rows[b, :, :, n0:n1], in_=y_sb[:, :, col : col + n1 - n0])
+                if i == rounds - 1:
+                    for b, n0, n1 in batch_parts(first, first + width):
+                        col = b * PIXELS + n0 - first
+                        nc.sync.dma_start(out=out_rows[b, :, m, n0:n1], in_=y_sb[:, m, col : col + n1 - n0])
+            if i < rounds - 1:
+                for b, n0, n1 in batch_parts(first, first + width):
+                    col = b * PIXELS + n0 - first
+                    nc.sync.dma_start(out=out_rows[b, :, :, n0:n1], in_=y_sb[:, :, col : col + n1 - n0])
 
         bw_f32 = keep.tile([P, M_TILES], F32)
         bn_scale = keep.tile([P, M_TILES], F32)
@@ -300,6 +327,7 @@ def tile_afnb_pb_t_kernel(tc, context, high_feats, ww, bw, wf, bfuse, gf, bef, m
         ww_grouped = transpose_weight(ww_sb, CV // K_PASS, "ww", nc.vector.tensor_copy)
         ww_codes, ww_scales = weight_tiles(CV // K_PASS, "ww")
         wf_codes, wf_scales = weight_tiles((CO + CH) // K_PASS, "wf")
+        spin(SPIN_NEXT)
         quantise_weight(ww_grouped, ww_codes, ww_scales)
         regroup_ctx(0)
         one_round(-1)

@@ -195,13 +195,6 @@ def tile_afnb_pb_t_kernel(tc, context, high_feats, ww, bw, wf, bfuse, gf, bef, m
             dst, src = by_runs(grouped_of["hi", i][:, split:width, :], raw_columns(hi_raw, i, split, width))
             nc.vector.tensor_copy(out=dst, in_=src)
 
-        def regroup_hi_scalar(i):
-            width = chunks[i][1]
-            grouped = work.tile([P, CHUNK, PACK], BF16, align_bytes=64, name="ctx_grouped", bufs=3)
-            dst, src = by_runs(grouped[:, :width, :], raw_columns(hi_raw, i, 0, width))
-            nc.scalar.copy(out=dst, in_=src)
-            grouped_of["hi", i] = grouped
-
         def quantise_chunk(operand, i, bufs):
             if not 0 <= i < rounds:
                 return
@@ -306,23 +299,17 @@ def tile_afnb_pb_t_kernel(tc, context, high_feats, ww, bw, wf, bfuse, gf, bef, m
             quantise_weight(wf_grouped, wf_codes, wf_scales)
 
         def one_round(i):
-            if i < rounds - 1:
-                regroup_hi_gpsimd(i)
+            regroup_hi_gpsimd(i)
             drain_c(i)
             second_product(i - 1)
-            if i < rounds - 1:
-                regroup_hi_vector(i)
+            regroup_hi_vector(i)
             quantise_chunk("ctx", i + 1, 2)
             first_product(i + 1)
             quantise_chunk("c", i, 2)
             if i == 0:
                 prepare_second_product()
-            if i < rounds - 1:
-                quantise_chunk("hi", i, 2)
+            quantise_chunk("hi", i, 2)
             regroup_ctx(i + 2)
-            if i == rounds - 2:
-                regroup_hi_scalar(i + 1)
-                quantise_chunk("hi", i + 1, 2)
 
         ww_grouped = transpose_weight(ww_sb, CV // K_PASS, "ww", nc.vector.tensor_copy)
         ww_codes, ww_scales = weight_tiles(CV // K_PASS, "ww")

@@ -24,8 +24,8 @@ M_TILES = CO // P
 BLOCK = 128
 MAX_LOAD = 4 * CHUNK
 RUN = 4
-SPIN_FIRST = 6
-SPIN_NEXT = 8
+SPIN_FIRST = 4
+SPIN_NEXT = 5
 EPS = 1e-5
 
 FLOPS = 2 * COLS * (CO * CV + CO * (CO + CH))

from contextlib import ExitStack

import concourse.mybir as mybir
from concourse.masks import make_identity

F32 = mybir.dt.float32
BF16 = mybir.dt.bfloat16
U32 = mybir.dt.uint32
U8 = mybir.dt.uint8
FP8X4 = mybir.dt.float8_e4m3fn_x4
IDENTITY = mybir.ActivationFunctionType.Identity
MULT = mybir.AluOpType.mult
ADD = mybir.AluOpType.add

P = 128
PACK = 4
K_PASS = P * PACK

BATCH, PIXELS = 2, 48 * 72
CV, CH, CO = 512, 512, 512
COLS = BATCH * PIXELS
CHUNK = 512
M_TILES = CO // P
BLOCK = 128
MAX_LOAD = 4 * CHUNK
RUN = 4
SPIN_FIRST = 4
SPIN_NEXT = 5
EPS = 1e-5

FLOPS = 2 * COLS * (CO * CV + CO * (CO + CH))


def batch_parts(first, last):
    parts = []
    for b in range(BATCH):
        lo = max(first, b * PIXELS)
        hi = min(last, (b + 1) * PIXELS)
        if lo < hi:
            parts.append((b, lo - b * PIXELS, hi - b * PIXELS))
    return parts


def tile_afnb_pb_t_kernel(tc, context, high_feats, ww, bw, wf, bfuse, gf, bef, mf, vf, out):
    nc = tc.nc
    chunks = [(first, min(CHUNK, COLS - first)) for first in range(0, COLS, CHUNK)]
    rounds = len(chunks)

    ctx_rows = context.rearrange("b (p j) h w -> b p j (h w)", j=PACK)
    hi_rows = high_feats.rearrange("b (p j) h w -> b p j (h w)", j=PACK)
    out_rows = out.rearrange("b (p m) h w -> b p m (h w)", m=M_TILES)

    with ExitStack() as stack:
        keep = stack.enter_context(tc.tile_pool(name="keep", bufs=1))
        work = stack.enter_context(tc.tile_pool(name="work", bufs=2))
        psum = stack.enter_context(tc.psum_pool(name="psum", bufs=4))
        stack.enter_context(tc.manual_schedule())

        warm = keep.tile([P, 1], F32)
        nc.vector.memset(warm[:], 1.0)
        nc.scalar.sqrt(out=warm[:], in_=warm[:])

        def load_vector(vec, name):
            vec_sb = keep.tile([P, M_TILES], BF16, name=name)
            nc.sync.dma_start(out=vec_sb[:], in_=vec.rearrange("(p m) -> p m", m=M_TILES))
            return vec_sb

        ww_sb = keep.tile([P, M_TILES * CV], BF16)
        wf_sb = keep.tile([P, M_TILES * (CO + CH)], BF16)
        nc.sync.dma_start(out=ww_sb[:], in_=ww.rearrange("(p m) k -> p (m k)", m=M_TILES))

        load_starts = [0]
        first, load_width = CHUNK, CHUNK
        while first < COLS:
            load_starts.append(first)
            first += load_width
            load_width = min(2 * load_width, MAX_LOAD)
        ctx_raw, hi_raw = {}, {}
        wanted = [(0, 1, "wf", 0, 0)]
        for first, last in zip(load_starts, load_starts[1:] + [COLS]):
            wanted.append((first // CHUNK - 2, 2, "ctx_raw", first, last))
            wanted.append((first // CHUNK, 0, "hi_raw", first, last))
        for need, rank, name, first, last in sorted(wanted):
            if name == "wf":
                nc.sync.dma_start(out=wf_sb[:], in_=wf.rearrange("(p m) k -> p (m k)", m=M_TILES))
                gf_sb = load_vector(gf, "gf_sb")
                bfuse_sb = load_vector(bfuse, "bfuse_sb")
                mf_sb = load_vector(mf, "mf_sb")
                bef_sb = load_vector(bef, "bef_sb")
            else:
                raw, rows = (ctx_raw, ctx_rows) if name == "ctx_raw" else (hi_raw, hi_rows)
                raw[first] = keep.tile([P, PACK, last - first], BF16, name="%s_%d" % (name, first))
                for b, n0, n1 in batch_parts(first, last):
                    col = b * PIXELS + n0 - first
                    nc.sync.dma_start(out=raw[first][:, :, col : col + n1 - n0], in_=rows[b, :, :, n0:n1])
                if first == 0 and name == "ctx_raw":
                    bw_sb = load_vector(bw, "bw_sb")
                    vf_sb = load_vector(vf, "vf_sb")

        ident = keep.tile([P, P], F32)
        make_identity(nc, ident[:])

        zeros = keep.tile([P, CHUNK], BF16)
        nc.vector.memset(zeros[:], 0.0)

        def spin(count):
            idle = psum.tile([P, CHUNK], F32, name="idle", tag="c_acc")
            for k in range(count):
                nc.tensor.matmul(out=idle[:], lhsT=zeros[:, :P], rhs=zeros[:], start=True, stop=True)

        spin(SPIN_FIRST)

        def transpose_weight(w_sb, passes, name, copy_out):
            words = w_sb[:].bitcast(F32).rearrange("p (m g q u) -> p m g u q", m=M_TILES, g=passes, u=2)
            grouped = keep.tile([P, passes * M_TILES * P * PACK], BF16, align_bytes=64, name=name + "_grouped")
            pairs = grouped[:].bitcast(F32).rearrange("q (g m c u) -> q g m c u", g=passes, m=M_TILES, u=2)
            for g in range(passes):
                for m0 in range(0, M_TILES, 2):
                    bank = psum.tile([P, 2, 2, P], F32, name="w_bank", tag="y_acc")
                    for i in range(2):
                        for u in range(2):
                            nc.tensor.transpose(bank[:, i, u, :], words[:, m0 + i, g, u, :], ident[:])
                    copy_out(out=pairs[:, g, m0 : m0 + 2], in_=bank[:].rearrange("q i u c -> q i c u"))
            return grouped

        def weight_tiles(passes, name):
            codes = keep.tile([P, passes, M_TILES, P], U32, align_bytes=64, name=name + "_codes")
            scales = keep.tile([P, passes, M_TILES, P], U8, align_bytes=64, name=name + "_scales")
            return codes, scales

        def quantise_weight(grouped, codes, scales):
            nc.vector.quantize_mx(
                out=codes[:].rearrange("q g m c -> q (g m c)").bitcast(FP8X4),
                scales=scales[:].rearrange("q g m c -> q (g m c)"),
                in_=grouped[:],
            )

        grouped_of = {}
        codes_of = {}
        c_banks = {}

        def raw_columns(raw, i, lo, hi):
            first = chunks[i][0]
            load = max(start for start in load_starts if start <= first)
            return raw[load][:, :, first - load + lo : first - load + hi]

        def by_runs(grouped, planes):
            return (
                grouped.rearrange("p (c i) t -> p c t i", i=RUN),
                planes.rearrange("p t (c i) -> p c t i", i=RUN),
            )

        def regroup_ctx(i):
            if not 0 <= i < rounds:
                return
            width = chunks[i][1]
            grouped = work.tile([P, CHUNK, PACK], BF16, align_bytes=64, name="ctx_grouped", bufs=3)
            split = width * 5 // 8 if i == 0 else width
            dst, src = by_runs(grouped[:, :split, :], raw_columns(ctx_raw, i, 0, split))
            nc.scalar.copy(out=dst, in_=src)
            if split < width:
                nc.gpsimd.tensor_scalar(
                    out=grouped[:, split:width, :],
                    in0=raw_columns(ctx_raw, i, split, width).rearrange("p t n -> p n t"),
                    scalar1=1.0,
                    scalar2=0.0,
                    op0=MULT,
                    op1=ADD,
                )
            grouped_of["ctx", i] = grouped

        def regroup_hi_gpsimd(i):
            if not 0 <= i < rounds:
                return
            width = chunks[i][1]
            split = width * 3 // 4
            grouped = work.tile([P, CHUNK, PACK], BF16, align_bytes=64, name="hi_grouped", bufs=1)
            if i == 0:
                nc.vector.memset(grouped[:, 0:1, :], 0.0)
            nc.gpsimd.tensor_scalar(
                out=grouped[:, :split, :],
                in0=raw_columns(hi_raw, i, 0, split).rearrange("p t n -> p n t"),
                scalar1=1.0,
                scalar2=0.0,
                op0=MULT,
                op1=ADD,
            )
            grouped_of["hi", i] = grouped

        def regroup_hi_vector(i):
            if not 0 <= i < rounds:
                return
            width = chunks[i][1]
            split = width * 3 // 4
            dst, src = by_runs(grouped_of["hi", i][:, split:width, :], raw_columns(hi_raw, i, split, width))
            nc.vector.tensor_copy(out=dst, in_=src)

        def quantise_chunk(operand, i, bufs):
            if not 0 <= i < rounds:
                return
            width = chunks[i][1]
            codes = work.tile([P, CHUNK], U32, align_bytes=64, name=operand + "_codes", bufs=bufs)
            scales = work.tile([P, CHUNK], U8, align_bytes=64, name=operand + "_scales", bufs=bufs)
            nc.vector.quantize_mx(
                out=codes[:, :width].bitcast(FP8X4),
                scales=scales[:, :width],
                in_=grouped_of[operand, i][:, :width, :].rearrange("p n t -> p (n t)"),
            )
            codes_of[operand, i] = (codes, scales)

        def first_product(i):
            if not 0 <= i < rounds:
                return
            width = chunks[i][1]
            ctx_codes, ctx_scales = codes_of["ctx", i]
            c_banks[i] = []
            for n0 in range(0, width, BLOCK):
                bank = psum.tile([P, M_TILES, BLOCK], F32, name="c_acc")
                for m in range(M_TILES):
                    nc.tensor.matmul_mx(
                        out=bank[:, m, :],
                        lhsT=ww_codes[:, 0, m, :].bitcast(FP8X4),
                        lhsT_scale=ww_scales[:, 0, m, :],
                        rhs=ctx_codes[:, n0 : n0 + BLOCK].bitcast(FP8X4),
                        rhs_scale=ctx_scales[:, n0 : n0 + BLOCK],
                        start=True,
                        stop=True,
                    )
                c_banks[i].append(bank)

        def drain_c(i):
            if not 0 <= i < rounds:
                return
            grouped = work.tile([P, CHUNK, PACK], BF16, align_bytes=64, name="c_grouped")
            for k, bank in enumerate(c_banks[i]):
                nc.vector.tensor_tensor(
                    out=grouped[:, k * BLOCK : (k + 1) * BLOCK, :],
                    in0=bank[:].rearrange("p m n -> p n m"),
                    in1=bw_f32[:].unsqueeze(1).to_broadcast([P, BLOCK, M_TILES]),
                    op=ADD,
                )
            grouped_of["c", i] = grouped

        def second_product(i):
            if not 0 <= i < rounds:
                return
            first, width = chunks[i]
            moving = [codes_of["c", i], codes_of["hi", i]]
            vector_helps = i == rounds - 1
            y_sb = work.tile([P, M_TILES, CHUNK], F32, bufs=6)
            for m in range(M_TILES):
                y_acc = psum.tile([P, CHUNK], F32)
                for g in range(len(moving)):
                    nc.tensor.matmul_mx(
                        out=y_acc[:, :width],
                        lhsT=wf_codes[:, g, m, :].bitcast(FP8X4),
                        lhsT_scale=wf_scales[:, g, m, :],
                        rhs=moving[g][0][:, :width].bitcast(FP8X4),
                        rhs_scale=moving[g][1][:, :width],
                        start=(g == 0),
                        stop=(g == len(moving) - 1),
                    )
                if vector_helps and m % 2 == 1:
                    nc.vector.tensor_scalar(
                        out=y_sb[:, m, :width],
                        in0=y_acc[:, :width],
                        scalar1=bn_scale[:, m : m + 1],
                        scalar2=bn_shift[:, m : m + 1],
                        op0=MULT,
                        op1=ADD,
                    )
                else:
                    nc.scalar.activation(
                        out=y_sb[:, m, :width],
                        in_=y_acc[:, :width],
                        func=IDENTITY,
                        scale=bn_scale[:, m : m + 1],
                        bias=bn_shift[:, m : m + 1],
                    )
                if i == rounds - 1:
                    for b, n0, n1 in batch_parts(first, first + width):
                        col = b * PIXELS + n0 - first
                        nc.sync.dma_start(out=out_rows[b, :, m, n0:n1], in_=y_sb[:, m, col : col + n1 - n0])
            if i < rounds - 1:
                for b, n0, n1 in batch_parts(first, first + width):
                    col = b * PIXELS + n0 - first
                    nc.sync.dma_start(out=out_rows[b, :, :, n0:n1], in_=y_sb[:, :, col : col + n1 - n0])

        bw_f32 = keep.tile([P, M_TILES], F32)
        bn_scale = keep.tile([P, M_TILES], F32)
        bn_shift = keep.tile([P, M_TILES], F32)

        def prepare_second_product():
            nc.vector.reciprocal(out=bn_scale[:], in_=bn_scale[:])
            nc.vector.tensor_mul(out=bn_scale[:], in0=bn_scale[:], in1=gf_sb[:])
            nc.vector.tensor_sub(out=bn_shift[:], in0=bfuse_sb[:], in1=mf_sb[:])
            nc.vector.tensor_mul(out=bn_shift[:], in0=bn_shift[:], in1=bn_scale[:])
            nc.vector.tensor_add(out=bn_shift[:], in0=bn_shift[:], in1=bef_sb[:])
            quantise_weight(wf_grouped, wf_codes, wf_scales)

        def one_round(i):
            regroup_hi_gpsimd(i)
            drain_c(i)
            second_product(i - 1)
            regroup_hi_vector(i)
            quantise_chunk("ctx", i + 1, 2)
            first_product(i + 1)
            quantise_chunk("c", i, 2)
            if i == 0:
                prepare_second_product()
            quantise_chunk("hi", i, 2)
            regroup_ctx(i + 2)

        ww_grouped = transpose_weight(ww_sb, CV // K_PASS, "ww", nc.vector.tensor_copy)
        ww_codes, ww_scales = weight_tiles(CV // K_PASS, "ww")
        wf_codes, wf_scales = weight_tiles((CO + CH) // K_PASS, "wf")
        spin(SPIN_NEXT)
        quantise_weight(ww_grouped, ww_codes, ww_scales)
        regroup_ctx(0)
        one_round(-1)
        nc.vector.tensor_copy(out=bw_f32[:], in_=bw_sb[:])
        nc.vector.tensor_scalar_add(out=bn_scale[:], in0=vf_sb[:], scalar1=EPS)
        nc.scalar.sqrt(out=bn_scale[:], in_=bn_scale[:])
        wf_grouped = transpose_weight(wf_sb, (CO + CH) // K_PASS, "wf", nc.scalar.copy)
        for i in range(rounds + 1):
            one_round(i)
